import numpy as np
import ml_dtypes

BF16 = ml_dtypes.bfloat16


def bf(x):
    return np.asarray(x, np.float32).astype(BF16)


def f32(x):
    return np.asarray(x, np.float32)


def f64(x):
    return np.asarray(x).astype(np.float64)


def striped(idx):
    return np.tile(idx.reshape(-1, 16).T, (8, 1))


D, S, B, N = 128, 256, 256, 512


def setup_inputs():
    return {"table": bf(0.1 * np.random.standard_normal((S, D))), "u": bf(np.random.standard_normal((D, B))), "kmem": bf(0.1 * np.random.standard_normal((D, N))), "val": bf(2.0 * np.random.standard_normal((N, D))), "offs": striped(np.random.permutation(np.tile(np.arange(S), 2))[:N])}


def reference(table, u, kmem, val, offs):
    idx = offs[:16].T.reshape(-1)
    logit = f64(u).T @ f64(table)[idx].T + f64(u).T @ f64(kmem)
    e = np.exp(logit)
    p = e / e.sum(axis=1, keepdims=True)
    return f64(u) + (p @ f64(val)).T

@@ -1,0 +1,84 @@
+import concourse.mybir as mybir
+from concourse.masks import make_identity
+
+P = 128
+D, S, B, N = 128, 256, 256, 512
+PIECE = 128
+BF16, F32, U16 = mybir.dt.bfloat16, mybir.dt.float32, mybir.dt.uint16
+EXP = mybir.ActivationFunctionType.Exp
+ADD = mybir.AluOpType.add
+FLOPS = 3 * 2 * B * N * D
+
+
+def tile_base_kernel(tc, table, u, kmem, val, offs, out):
+    nc = tc.nc
+    with (
+        tc.tile_pool(name="held", bufs=1) as held,
+        tc.tile_pool(name="work", bufs=2) as work,
+        tc.psum_pool(name="psum_once", bufs=1) as psum_once,
+        tc.psum_pool(name="psum", bufs=2) as psum,
+    ):
+        identity = held.tile([P, P], BF16, name="identity")
+        make_identity(nc, identity[:])
+
+        offsets = held.tile([P, N // 16], U16, name="offsets")
+        nc.sync.dma_start(offsets[:], offs)
+        table_rows = held.tile([P, S // P, D], BF16, name="table_rows")
+        nc.sync.dma_start(table_rows[:], table.rearrange("(h p) d -> p h d", p=P))
+        u_sb = held.tile([D, B], BF16, name="u_sb")
+        nc.scalar.dma_start(u_sb[:], u)
+        kmem_sb = held.tile([D, N], BF16, name="kmem_sb")
+        nc.scalar.dma_start(kmem_sb[:], kmem)
+        val_sb = held.tile([P, N // P, D], BF16, name="val_sb")
+        nc.sync.dma_start(val_sb[:], val.rearrange("(k p) d -> p k d", p=P))
+
+        blocks = range(B // P)
+        queries = [u_sb[:, blk * P : (blk + 1) * P] for blk in blocks]
+        logits = [psum.tile([P, N], F32, name="logit") for blk in blocks]
+        for blk in blocks:
+            nc.tensor.matmul(logits[blk][:], queries[blk], kmem_sb[:], start=True, stop=False)
+
+        table_cols_ps = psum_once.tile([D, S], BF16, name="table_cols_ps")
+        for h in range(S // P):
+            nc.tensor.transpose(table_cols_ps[:, h * P : (h + 1) * P], table_rows[:, h, :], identity[:])
+        table_cols = held.tile([D, S], BF16, name="table_cols")
+        nc.vector.tensor_copy(table_cols[:], table_cols_ps[:])
+
+        pieces = range(N // PIECE)
+        for blk in blocks:
+            for piece in pieces:
+                nc.tensor.matmul(
+                    logits[blk][:, piece * PIECE : (piece + 1) * PIECE],
+                    queries[blk],
+                    table_cols[:].indirect(offsets[:, piece * PIECE // 16 : (piece + 1) * PIECE // 16]),
+                    start=False,
+                    stop=(piece == pieces[-1]),
+                )
+
+        for blk in blocks:
+            logit = logits[blk]
+
+            neg_max = work.tile([P, 1], F32, name="neg_max")
+            nc.vector.reduce_max(neg_max[:], logit[:], axis=mybir.AxisListType.X, negate=True)
+            e = work.tile([P, N], F32, name="e")
+            z = work.tile([P, 1], F32, name="z")
+            nc.scalar.activation(e[:], logit[:], EXP, bias=neg_max[:], accum_out=z[:])
+            inv_z = work.tile([P, 1], F32, name="inv_z")
+            nc.vector.reciprocal(inv_z[:], z[:])
+            p = work.tile([P, N], BF16, name="p")
+            nc.vector.tensor_scalar_mul(p[:], e[:], inv_z[:])
+
+            p_flipped_ps = psum.tile([P, N // P, P], BF16, name="p_flipped_ps")
+            for k in range(N // P):
+                nc.tensor.transpose(p_flipped_ps[:, k, :], p[:, k * P : (k + 1) * P], identity[:])
+            p_flipped = work.tile([P, N // P, P], BF16, name="p_flipped")
+            nc.scalar.copy(p_flipped[:], p_flipped_ps[:])
+
+            read_out = psum.tile([D, P], F32, name="read_out")
+            for k in range(N // P):
+                nc.tensor.matmul(
+                    read_out[:], val_sb[:, k, :], p_flipped[:, k, :], start=(k == 0), stop=(k == N // P - 1)
+                )
+            out_sb = work.tile([D, P], F32, name="out_sb")
+            nc.vector.tensor_tensor(out_sb[:], read_out[:], queries[blk], ADD)
+            nc.sync.dma_start(out[:, blk * P : (blk + 1) * P], out_sb[:])

@@ -24,25 +24,25 @@ def tile_base_kernel(tc, table, u, kmem, val, offs, out):
         offsets = held.tile([P, N // 16], U16, name="offsets")
         nc.sync.dma_start(offsets[:], offs)
         table_rows = held.tile([P, S // P, D], BF16, name="table_rows")
-        nc.sync.dma_start(table_rows[:], table.rearrange("(h p) d -> p h d", p=P))
+        nc.scalar.dma_start(table_rows[:], table.rearrange("(h p) d -> p h d", p=P))
         u_sb = held.tile([D, B], BF16, name="u_sb")
-        nc.scalar.dma_start(u_sb[:], u)
+        nc.sync.dma_start(u_sb[:], u)
         kmem_sb = held.tile([D, N], BF16, name="kmem_sb")
         nc.scalar.dma_start(kmem_sb[:], kmem)
         val_sb = held.tile([P, N // P, D], BF16, name="val_sb")
         nc.sync.dma_start(val_sb[:], val.rearrange("(k p) d -> p k d", p=P))
-
-        blocks = range(B // P)
-        queries = [u_sb[:, blk * P : (blk + 1) * P] for blk in blocks]
-        logits = [psum.tile([P, N], F32, name="logit") for blk in blocks]
-        for blk in blocks:
-            nc.tensor.matmul(logits[blk][:], queries[blk], kmem_sb[:], start=True, stop=False)
 
         table_cols_ps = psum_once.tile([D, S], BF16, name="table_cols_ps")
         for h in range(S // P):
             nc.tensor.transpose(table_cols_ps[:, h * P : (h + 1) * P], table_rows[:, h, :], identity[:])
         table_cols = held.tile([D, S], BF16, name="table_cols")
         nc.vector.tensor_copy(table_cols[:], table_cols_ps[:])
+
+        blocks = range(B // P)
+        queries = [u_sb[:, blk * P : (blk + 1) * P] for blk in blocks]
+        logits = [psum.tile([P, N], F32, name="logit") for blk in blocks]
+        for blk in blocks:
+            nc.tensor.matmul(logits[blk][:], queries[blk], kmem_sb[:], start=True, stop=False)
 
         pieces = range(N // PIECE)
         for blk in blocks:

@@ -8,6 +8,7 @@ BF16, F32, U16 = mybir.dt.bfloat16, mybir.dt.float32, mybir.dt.uint16
 EXP = mybir.ActivationFunctionType.Exp
 ADD = mybir.AluOpType.add
 FLOPS = 3 * 2 * B * N * D
+WARM_UPS = 6
 
 
 def tile_base_kernel(tc, table, u, kmem, val, offs, out):
@@ -31,6 +32,12 @@ def tile_base_kernel(tc, table, u, kmem, val, offs, out):
         nc.scalar.dma_start(kmem_sb[:], kmem)
         val_sb = held.tile([P, N // P, D], BF16, name="val_sb")
         nc.sync.dma_start(val_sb[:], val.rearrange("(k p) d -> p k d", p=P))
+
+        zeros = held.tile([P, N], BF16, name="zeros")
+        nc.vector.memset(zeros[:], 0.0)
+        unread_ps = psum_once.tile([P, N], F32, name="unread_ps")
+        for i in range(WARM_UPS):
+            nc.tensor.matmul(unread_ps[:], zeros[:, 0:P], zeros[:], start=True, stop=True)
 
         table_cols_ps = psum_once.tile([D, S], BF16, name="table_cols_ps")
         for h in range(S // P):

@@ -8,7 +8,7 @@ BF16, F32, U16 = mybir.dt.bfloat16, mybir.dt.float32, mybir.dt.uint16
 EXP = mybir.ActivationFunctionType.Exp
 ADD = mybir.AluOpType.add
 FLOPS = 3 * 2 * B * N * D
-WARM_UPS = 6
+WARM_UPS = 16
 
 
 def tile_base_kernel(tc, table, u, kmem, val, offs, out):
@@ -19,6 +19,12 @@ def tile_base_kernel(tc, table, u, kmem, val, offs, out):
         tc.psum_pool(name="psum_once", bufs=1) as psum_once,
         tc.psum_pool(name="psum", bufs=2) as psum,
     ):
+        zeros = held.tile([P, P], BF16, name="zeros")
+        nc.gpsimd.memset(zeros[:], 0.0)
+        unread_ps = psum_once.tile([P, P], F32, name="unread_ps")
+        for i in range(WARM_UPS):
+            nc.tensor.matmul(unread_ps[:], zeros[:], zeros[:], start=True, stop=True)
+
         identity = held.tile([P, P], BF16, name="identity")
         make_identity(nc, identity[:])
 
@@ -32,12 +38,6 @@ def tile_base_kernel(tc, table, u, kmem, val, offs, out):
         nc.scalar.dma_start(kmem_sb[:], kmem)
         val_sb = held.tile([P, N // P, D], BF16, name="val_sb")
         nc.sync.dma_start(val_sb[:], val.rearrange("(k p) d -> p k d", p=P))
-
-        zeros = held.tile([P, N], BF16, name="zeros")
-        nc.vector.memset(zeros[:], 0.0)
-        unread_ps = psum_once.tile([P, N], F32, name="unread_ps")
-        for i in range(WARM_UPS):
-            nc.tensor.matmul(unread_ps[:], zeros[:, 0:P], zeros[:], start=True, stop=True)
 
         table_cols_ps = psum_once.tile([D, S], BF16, name="table_cols_ps")
         for h in range(S // P):

@@ -9,6 +9,7 @@ EXP = mybir.ActivationFunctionType.Exp
 ADD = mybir.AluOpType.add
 FLOPS = 3 * 2 * B * N * D
 WARM_UPS = 16
+LULL_FILLS = 4
 
 
 def tile_base_kernel(tc, table, u, kmem, val, offs, out):
@@ -21,9 +22,9 @@ def tile_base_kernel(tc, table, u, kmem, val, offs, out):
     ):
         zeros = held.tile([P, P], BF16, name="zeros")
         nc.gpsimd.memset(zeros[:], 0.0)
-        unread_ps = psum_once.tile([P, P], F32, name="unread_ps")
+        unread_ps = psum_once.tile([P, N], F32, name="unread_ps")
         for i in range(WARM_UPS):
-            nc.tensor.matmul(unread_ps[:], zeros[:], zeros[:], start=True, stop=True)
+            nc.tensor.matmul(unread_ps[:, 0:P], zeros[:], zeros[:], start=True, stop=True)
 
         identity = held.tile([P, P], BF16, name="identity")
         make_identity(nc, identity[:])
@@ -62,6 +63,9 @@ def tile_base_kernel(tc, table, u, kmem, val, offs, out):
                     stop=(piece == pieces[-1]),
                 )
 
+        for i in range(LULL_FILLS):
+            nc.tensor.matmul(unread_ps[:, 0:S], zeros[:], table_cols[:], start=True, stop=True)
+
         for blk in blocks:
             logit = logits[blk]
 
@@ -78,6 +82,8 @@ def tile_base_kernel(tc, table, u, kmem, val, offs, out):
             p_flipped_ps = psum.tile([P, N // P, P], BF16, name="p_flipped_ps")
             for k in range(N // P):
                 nc.tensor.transpose(p_flipped_ps[:, k, :], p[:, k * P : (k + 1) * P], identity[:])
+            if blk < blocks[-1]:
+                nc.tensor.matmul(unread_ps[:], zeros[:], p[:], start=True, stop=True)
             p_flipped = work.tile([P, N // P, P], BF16, name="p_flipped")
             nc.scalar.copy(p_flipped[:], p_flipped_ps[:])
 

@@ -47,21 +47,20 @@ def tile_base_kernel(tc, table, u, kmem, val, offs, out):
         nc.vector.tensor_copy(table_cols[:], table_cols_ps[:])
 
         blocks = range(B // P)
+        pieces = range(N // PIECE)
         queries = [u_sb[:, blk * P : (blk + 1) * P] for blk in blocks]
         logits = [psum.tile([P, N], F32, name="logit") for blk in blocks]
-        for blk in blocks:
-            nc.tensor.matmul(logits[blk][:], queries[blk], kmem_sb[:], start=True, stop=False)
-
-        pieces = range(N // PIECE)
+        nc.tensor.matmul(logits[0][:], queries[0], kmem_sb[:], start=True, stop=False)
         for blk in blocks:
             for piece in pieces:
                 nc.tensor.matmul(
                     logits[blk][:, piece * PIECE : (piece + 1) * PIECE],
                     queries[blk],
                     table_cols[:].indirect(offsets[:, piece * PIECE // 16 : (piece + 1) * PIECE // 16]),
-                    start=False,
-                    stop=(piece == pieces[-1]),
+                    start=(blk == 1 and piece == 0),
+                    stop=(blk == 0 and piece == pieces[-1]),
                 )
+        nc.tensor.matmul(logits[1][:], queries[1], kmem_sb[:], start=False, stop=True)
 
         for i in range(LULL_FILLS):
             nc.tensor.matmul(unread_ps[:, 0:S], zeros[:], table_cols[:], start=True, stop=True)

@@ -29,12 +29,12 @@ def tile_base_kernel(tc, table, u, kmem, val, offs, out):
         identity = held.tile([P, P], BF16, name="identity")
         make_identity(nc, identity[:])
 
-        offsets = held.tile([P, N // 16], U16, name="offsets")
-        nc.sync.dma_start(offsets[:], offs)
         table_rows = held.tile([P, S // P, D], BF16, name="table_rows")
-        nc.scalar.dma_start(table_rows[:], table.rearrange("(h p) d -> p h d", p=P))
+        nc.sync.dma_start(table_rows[:], table.rearrange("(h p) d -> p h d", p=P))
         u_sb = held.tile([D, B], BF16, name="u_sb")
         nc.sync.dma_start(u_sb[:], u)
+        offsets = held.tile([P, N // 16], U16, name="offsets")
+        nc.sync.dma_start(offsets[:], offs)
         kmem_sb = held.tile([D, N], BF16, name="kmem_sb")
         nc.scalar.dma_start(kmem_sb[:], kmem)
         val_sb = held.tile([P, N // P, D], BF16, name="val_sb")

@@ -4,6 +4,7 @@ from concourse.masks import make_identity
 P = 128
 D, S, B, N = 128, 256, 256, 512
 PIECE = 128
+HALF = N // 2
 BF16, F32, U16 = mybir.dt.bfloat16, mybir.dt.float32, mybir.dt.uint16
 EXP = mybir.ActivationFunctionType.Exp
 ADD = mybir.AluOpType.add
@@ -48,6 +49,7 @@ def tile_base_kernel(tc, table, u, kmem, val, offs, out):
 
         blocks = range(B // P)
         pieces = range(N // PIECE)
+        halves = range(N // HALF)
         queries = [u_sb[:, blk * P : (blk + 1) * P] for blk in blocks]
         logits = [psum.tile([P, N], F32, name="logit") for blk in blocks]
         nc.tensor.matmul(logits[0][:], queries[0], kmem_sb[:], start=True, stop=False)
@@ -75,22 +77,30 @@ def tile_base_kernel(tc, table, u, kmem, val, offs, out):
             nc.scalar.activation(e[:], logit[:], EXP, bias=neg_max[:], accum_out=z[:])
             inv_z = work.tile([P, 1], F32, name="inv_z")
             nc.vector.reciprocal(inv_z[:], z[:])
-            p = work.tile([P, N], BF16, name="p")
-            nc.vector.tensor_scalar_mul(p[:], e[:], inv_z[:])
+            p = [work.tile([P, HALF], BF16, name=f"p{half}") for half in halves]
+            for half in halves:
+                nc.vector.tensor_scalar_mul(p[half][:], e[:, half * HALF : (half + 1) * HALF], inv_z[:])
 
-            p_flipped_ps = psum.tile([P, N // P, P], BF16, name="p_flipped_ps")
-            for k in range(N // P):
-                nc.tensor.transpose(p_flipped_ps[:, k, :], p[:, k * P : (k + 1) * P], identity[:])
+            p_flipped_ps = [psum_once.tile([P, HALF // P, P], BF16, name=f"p_flipped_ps{half}") for half in halves]
+            for half in halves:
+                for k in range(HALF // P):
+                    nc.tensor.transpose(p_flipped_ps[half][:, k, :], p[half][:, k * P : (k + 1) * P], identity[:])
             if blk < blocks[-1]:
-                nc.tensor.matmul(unread_ps[:], zeros[:], p[:], start=True, stop=True)
-            p_flipped = work.tile([P, N // P, P], BF16, name="p_flipped")
-            nc.scalar.copy(p_flipped[:], p_flipped_ps[:])
+                nc.tensor.matmul(unread_ps[:, 0:HALF], zeros[:], p[1][:], start=True, stop=True)
+            p_flipped = [work.tile([P, HALF // P, P], BF16, name=f"p_flipped{half}") for half in halves]
+            nc.scalar.copy(p_flipped[0][:], p_flipped_ps[0][:])
+            nc.vector.tensor_copy(p_flipped[1][:], p_flipped_ps[1][:])
 
             read_out = psum.tile([D, P], F32, name="read_out")
-            for k in range(N // P):
-                nc.tensor.matmul(
-                    read_out[:], val_sb[:, k, :], p_flipped[:, k, :], start=(k == 0), stop=(k == N // P - 1)
-                )
+            for half in halves:
+                for k in range(HALF // P):
+                    nc.tensor.matmul(
+                        read_out[:],
+                        val_sb[:, half * (HALF // P) + k, :],
+                        p_flipped[half][:, k, :],
+                        start=(half == 0 and k == 0),
+                        stop=(half == halves[-1] and k == HALF // P - 1),
+                    )
             out_sb = work.tile([D, P], F32, name="out_sb")
             nc.vector.tensor_tensor(out_sb[:], read_out[:], queries[blk], ADD)
             nc.sync.dma_start(out[:, blk * P : (blk + 1) * P], out_sb[:])

@@ -10,7 +10,7 @@ EXP = mybir.ActivationFunctionType.Exp
 ADD = mybir.AluOpType.add
 FLOPS = 3 * 2 * B * N * D
 WARM_UPS = 16
-LULL_FILLS = 4
+LULL_FILLS = 10
 
 
 def tile_base_kernel(tc, table, u, kmem, val, offs, out):
@@ -86,7 +86,8 @@ def tile_base_kernel(tc, table, u, kmem, val, offs, out):
                 for k in range(HALF // P):
                     nc.tensor.transpose(p_flipped_ps[half][:, k, :], p[half][:, k * P : (k + 1) * P], identity[:])
             if blk < blocks[-1]:
-                nc.tensor.matmul(unread_ps[:, 0:HALF], zeros[:], p[1][:], start=True, stop=True)
+                for half in halves:
+                    nc.tensor.matmul(unread_ps[:, 0:HALF], zeros[:], p[half][:], start=True, stop=True)
             p_flipped = [work.tile([P, HALF // P, P], BF16, name=f"p_flipped{half}") for half in halves]
             nc.scalar.copy(p_flipped[0][:], p_flipped_ps[0][:])
             nc.vector.tensor_copy(p_flipped[1][:], p_flipped_ps[1][:])

@@ -18,12 +18,11 @@ def tile_base_kernel(tc, table, u, kmem, val, offs, out):
     with (
         tc.tile_pool(name="held", bufs=1) as held,
         tc.tile_pool(name="work", bufs=2) as work,
-        tc.psum_pool(name="psum_once", bufs=1) as psum_once,
         tc.psum_pool(name="psum", bufs=2) as psum,
     ):
         zeros = held.tile([P, P], BF16, name="zeros")
         nc.gpsimd.memset(zeros[:], 0.0)
-        unread_ps = psum_once.tile([P, N], F32, name="unread_ps")
+        unread_ps = psum.tile([P, N], F32, name="unread_ps", tag="read_out")
         for i in range(WARM_UPS):
             nc.tensor.matmul(unread_ps[:, 0:P], zeros[:], zeros[:], start=True, stop=True)
 
@@ -41,7 +40,7 @@ def tile_base_kernel(tc, table, u, kmem, val, offs, out):
         val_sb = held.tile([P, N // P, D], BF16, name="val_sb")
         nc.sync.dma_start(val_sb[:], val.rearrange("(k p) d -> p k d", p=P))
 
-        table_cols_ps = psum_once.tile([D, S], BF16, name="table_cols_ps")
+        table_cols_ps = psum.tile([D, S], BF16, name="table_cols_ps", tag="flipped_ps0")
         for h in range(S // P):
             nc.tensor.transpose(table_cols_ps[:, h * P : (h + 1) * P], table_rows[:, h, :], identity[:])
         table_cols = held.tile([D, S], BF16, name="table_cols")
@@ -81,7 +80,9 @@ def tile_base_kernel(tc, table, u, kmem, val, offs, out):
             for half in halves:
                 nc.vector.tensor_scalar_mul(p[half][:], e[:, half * HALF : (half + 1) * HALF], inv_z[:])
 
-            p_flipped_ps = [psum_once.tile([P, HALF // P, P], BF16, name=f"p_flipped_ps{half}") for half in halves]
+            p_flipped_ps = [
+                psum.tile([P, HALF // P, P], BF16, name=f"p_flipped_ps{half}", tag=f"flipped_ps{half}") for half in halves
+            ]
             for half in halves:
                 for k in range(HALF // P):
                     nc.tensor.transpose(p_flipped_ps[half][:, k, :], p[half][:, k * P : (k + 1) * P], identity[:])
@@ -90,7 +91,10 @@ def tile_base_kernel(tc, table, u, kmem, val, offs, out):
                     nc.tensor.matmul(unread_ps[:, 0:HALF], zeros[:], p[half][:], start=True, stop=True)
             p_flipped = [work.tile([P, HALF // P, P], BF16, name=f"p_flipped{half}") for half in halves]
             nc.scalar.copy(p_flipped[0][:], p_flipped_ps[0][:])
-            nc.vector.tensor_copy(p_flipped[1][:], p_flipped_ps[1][:])
+            if blk < blocks[-1]:
+                nc.scalar.copy(p_flipped[1][:], p_flipped_ps[1][:])
+            else:
+                nc.vector.tensor_copy(p_flipped[1][:], p_flipped_ps[1][:])
 
             read_out = psum.tile([D, P], F32, name="read_out")
             for half in halves:

@@ -90,11 +90,11 @@ def tile_base_kernel(tc, table, u, kmem, val, offs, out):
                 for half in halves:
                     nc.tensor.matmul(unread_ps[:, 0:HALF], zeros[:], p[half][:], start=True, stop=True)
             p_flipped = [work.tile([P, HALF // P, P], BF16, name=f"p_flipped{half}") for half in halves]
-            nc.scalar.copy(p_flipped[0][:], p_flipped_ps[0][:])
-            if blk < blocks[-1]:
-                nc.scalar.copy(p_flipped[1][:], p_flipped_ps[1][:])
-            else:
-                nc.vector.tensor_copy(p_flipped[1][:], p_flipped_ps[1][:])
+            for half in halves:
+                if blk < blocks[-1]:
+                    nc.scalar.copy(p_flipped[half][:], p_flipped_ps[half][:])
+                else:
+                    nc.vector.tensor_copy(p_flipped[half][:], p_flipped_ps[half][:])
 
             read_out = psum.tile([D, P], F32, name="read_out")
             for half in halves:

@@ -4,7 +4,6 @@ from concourse.masks import make_identity
 P = 128
 D, S, B, N = 128, 256, 256, 512
 PIECE = 128
-HALF = N // 2
 BF16, F32, U16 = mybir.dt.bfloat16, mybir.dt.float32, mybir.dt.uint16
 EXP = mybir.ActivationFunctionType.Exp
 ADD = mybir.AluOpType.add
@@ -18,11 +17,11 @@ def tile_base_kernel(tc, table, u, kmem, val, offs, out):
     with (
         tc.tile_pool(name="held", bufs=1) as held,
         tc.tile_pool(name="work", bufs=2) as work,
-        tc.psum_pool(name="psum", bufs=2) as psum,
+        tc.psum_pool(name="psum", bufs=8) as psum,
     ):
         zeros = held.tile([P, P], BF16, name="zeros")
         nc.gpsimd.memset(zeros[:], 0.0)
-        unread_ps = psum.tile([P, N], F32, name="unread_ps", tag="read_out")
+        unread_ps = psum.tile([P, N], F32, name="unread_ps", tag="bank")
         for i in range(WARM_UPS):
             nc.tensor.matmul(unread_ps[:, 0:P], zeros[:], zeros[:], start=True, stop=True)
 
@@ -40,7 +39,7 @@ def tile_base_kernel(tc, table, u, kmem, val, offs, out):
         val_sb = held.tile([P, N // P, D], BF16, name="val_sb")
         nc.sync.dma_start(val_sb[:], val.rearrange("(k p) d -> p k d", p=P))
 
-        table_cols_ps = psum.tile([D, S], BF16, name="table_cols_ps", tag="flipped_ps0")
+        table_cols_ps = psum.tile([D, S], BF16, name="table_cols_ps", tag="bank")
         for h in range(S // P):
             nc.tensor.transpose(table_cols_ps[:, h * P : (h + 1) * P], table_rows[:, h, :], identity[:])
         table_cols = held.tile([D, S], BF16, name="table_cols")
@@ -48,9 +47,8 @@ def tile_base_kernel(tc, table, u, kmem, val, offs, out):
 
         blocks = range(B // P)
         pieces = range(N // PIECE)
-        halves = range(N // HALF)
         queries = [u_sb[:, blk * P : (blk + 1) * P] for blk in blocks]
-        logits = [psum.tile([P, N], F32, name="logit") for blk in blocks]
+        logits = [psum.tile([P, N], F32, name="logit", tag="bank") for blk in blocks]
         nc.tensor.matmul(logits[0][:], queries[0], kmem_sb[:], start=True, stop=False)
         for blk in blocks:
             for piece in pieces:
@@ -76,35 +74,37 @@ def tile_base_kernel(tc, table, u, kmem, val, offs, out):
             nc.scalar.activation(e[:], logit[:], EXP, bias=neg_max[:], accum_out=z[:])
             inv_z = work.tile([P, 1], F32, name="inv_z")
             nc.vector.reciprocal(inv_z[:], z[:])
-            p = [work.tile([P, HALF], BF16, name=f"p{half}") for half in halves]
-            for half in halves:
-                nc.vector.tensor_scalar_mul(p[half][:], e[:, half * HALF : (half + 1) * HALF], inv_z[:])
+            chunks = 2 if blk < blocks[-1] else 1
+            width = chunks * P
+            parts = range(N // width)
+            p = [work.tile([P, width], BF16, name=f"p{part}") for part in parts]
+            for part in parts:
+                nc.vector.tensor_scalar_mul(p[part][:], e[:, part * width : (part + 1) * width], inv_z[:])
 
-            p_flipped_ps = [
-                psum.tile([P, HALF // P, P], BF16, name=f"p_flipped_ps{half}", tag=f"flipped_ps{half}") for half in halves
-            ]
-            for half in halves:
-                for k in range(HALF // P):
-                    nc.tensor.transpose(p_flipped_ps[half][:, k, :], p[half][:, k * P : (k + 1) * P], identity[:])
+            p_flipped_ps = [psum.tile([P, chunks, P], BF16, name=f"p_flipped_ps{part}", tag="bank") for part in parts]
+            for part in parts:
+                for k in range(chunks):
+                    nc.tensor.transpose(p_flipped_ps[part][:, k, :], p[part][:, k * P : (k + 1) * P], identity[:])
             if blk < blocks[-1]:
-                for half in halves:
-                    nc.tensor.matmul(unread_ps[:, 0:HALF], zeros[:], p[half][:], start=True, stop=True)
-            p_flipped = [work.tile([P, HALF // P, P], BF16, name=f"p_flipped{half}") for half in halves]
-            for half in halves:
+                for part in parts:
+                    nc.tensor.matmul(unread_ps[:, 0:width], zeros[:], p[part][:], start=True, stop=True)
+            p_flipped = [work.tile([P, chunks, P], BF16, name=f"p_flipped{part}") for part in parts]
+            for part in parts:
                 if blk < blocks[-1]:
-                    nc.scalar.copy(p_flipped[half][:], p_flipped_ps[half][:])
+                    nc.scalar.copy(p_flipped[part][:], p_flipped_ps[part][:])
                 else:
-                    nc.vector.tensor_copy(p_flipped[half][:], p_flipped_ps[half][:])
+                    nc.vector.tensor_copy(p_flipped[part][:], p_flipped_ps[part][:])
 
-            read_out = psum.tile([D, P], F32, name="read_out")
-            for half in halves:
-                for k in range(HALF // P):
+            read_out = psum.tile([D, P], F32, name="read_out", tag="bank")
+            for part in parts:
+                for k in range(chunks):
+                    chunk = part * chunks + k
                     nc.tensor.matmul(
                         read_out[:],
-                        val_sb[:, half * (HALF // P) + k, :],
-                        p_flipped[half][:, k, :],
-                        start=(half == 0 and k == 0),
-                        stop=(half == halves[-1] and k == HALF // P - 1),
+                        val_sb[:, chunk, :],
+                        p_flipped[part][:, k, :],
+                        start=(chunk == 0),
+                        stop=(chunk == N // P - 1),
                     )
             out_sb = work.tile([D, P], F32, name="out_sb")
             nc.vector.tensor_tensor(out_sb[:], read_out[:], queries[blk], ADD)

@@ -8,8 +8,8 @@ BF16, F32, U16 = mybir.dt.bfloat16, mybir.dt.float32, mybir.dt.uint16
 EXP = mybir.ActivationFunctionType.Exp
 ADD = mybir.AluOpType.add
 FLOPS = 3 * 2 * B * N * D
-WARM_UPS = 16
-LULL_FILLS = 10
+WARM_UPS = 4
+LULL_FILLS = 5
 
 
 def tile_base_kernel(tc, table, u, kmem, val, offs, out):
@@ -19,11 +19,13 @@ def tile_base_kernel(tc, table, u, kmem, val, offs, out):
         tc.tile_pool(name="work", bufs=2) as work,
         tc.psum_pool(name="psum", bufs=8) as psum,
     ):
-        zeros = held.tile([P, P], BF16, name="zeros")
-        nc.gpsimd.memset(zeros[:], 0.0)
+        zero_column = held.tile([P, 1], BF16, name="zero_column")
+        nc.gpsimd.memset(zero_column[:], 0.0)
+        zero_weights = zero_column[:].to_broadcast([P, P])
+        zero_columns = zero_column[:].to_broadcast([P, N])
         unread_ps = psum.tile([P, N], F32, name="unread_ps", tag="bank")
         for i in range(WARM_UPS):
-            nc.tensor.matmul(unread_ps[:, 0:P], zeros[:], zeros[:], start=True, stop=True)
+            nc.tensor.matmul(unread_ps[:], zero_weights, zero_columns, start=True, stop=True)
 
         identity = held.tile([P, P], BF16, name="identity")
         make_identity(nc, identity[:])
@@ -62,7 +64,7 @@ def tile_base_kernel(tc, table, u, kmem, val, offs, out):
         nc.tensor.matmul(logits[1][:], queries[1], kmem_sb[:], start=False, stop=True)
 
         for i in range(LULL_FILLS):
-            nc.tensor.matmul(unread_ps[:, 0:S], zeros[:], table_cols[:], start=True, stop=True)
+            nc.tensor.matmul(unread_ps[:], table_cols[:, 0:P], zero_columns, start=True, stop=True)
 
         for blk in blocks:
             logit = logits[blk]
@@ -86,8 +88,7 @@ def tile_base_kernel(tc, table, u, kmem, val, offs, out):
                 for k in range(chunks):
                     nc.tensor.transpose(p_flipped_ps[part][:, k, :], p[part][:, k * P : (k + 1) * P], identity[:])
             if blk < blocks[-1]:
-                for part in parts:
-                    nc.tensor.matmul(unread_ps[:, 0:width], zeros[:], p[part][:], start=True, stop=True)
+                nc.tensor.matmul(unread_ps[:], p[parts[-1]][:, 0:P], zero_columns, start=True, stop=True)
             p_flipped = [work.tile([P, chunks, P], BF16, name=f"p_flipped{part}") for part in parts]
             for part in parts:
                 if blk < blocks[-1]:

@@ -17,13 +17,14 @@ def tile_base_kernel(tc, table, u, kmem, val, offs, out):
     with (
         tc.tile_pool(name="held", bufs=1) as held,
         tc.tile_pool(name="work", bufs=2) as work,
-        tc.psum_pool(name="psum", bufs=8) as psum,
+        tc.psum_pool(name="psum", bufs=7) as psum,
+        tc.psum_pool(name="psum_unread", bufs=1) as psum_unread,
     ):
         zero_column = held.tile([P, 1], BF16, name="zero_column")
         nc.gpsimd.memset(zero_column[:], 0.0)
         zero_weights = zero_column[:].to_broadcast([P, P])
         zero_columns = zero_column[:].to_broadcast([P, N])
-        unread_ps = psum.tile([P, N], F32, name="unread_ps", tag="bank")
+        unread_ps = psum_unread.tile([P, N], F32, name="unread_ps", tag="bank")
         for i in range(WARM_UPS):
             nc.tensor.matmul(unread_ps[:], zero_weights, zero_columns, start=True, stop=True)
 
@@ -66,37 +67,47 @@ def tile_base_kernel(tc, table, u, kmem, val, offs, out):
         for i in range(LULL_FILLS):
             nc.tensor.matmul(unread_ps[:], table_cols[:, 0:P], zero_columns, start=True, stop=True)
 
+        chunks_in_part = [2, 1]
+        p_flipped_ps = []
         for blk in blocks:
-            logit = logits[blk]
-
             neg_max = work.tile([P, 1], F32, name="neg_max")
-            nc.vector.reduce_max(neg_max[:], logit[:], axis=mybir.AxisListType.X, negate=True)
+            nc.vector.reduce_max(neg_max[:], logits[blk][:], axis=mybir.AxisListType.X, negate=True)
             e = work.tile([P, N], F32, name="e")
             z = work.tile([P, 1], F32, name="z")
-            nc.scalar.activation(e[:], logit[:], EXP, bias=neg_max[:], accum_out=z[:])
+            nc.scalar.activation(e[:], logits[blk][:], EXP, bias=neg_max[:], accum_out=z[:])
             inv_z = work.tile([P, 1], F32, name="inv_z")
             nc.vector.reciprocal(inv_z[:], z[:])
-            chunks = 2 if blk < blocks[-1] else 1
+            chunks = chunks_in_part[blk]
             width = chunks * P
             parts = range(N // width)
             p = [work.tile([P, width], BF16, name=f"p{part}") for part in parts]
             for part in parts:
                 nc.vector.tensor_scalar_mul(p[part][:], e[:, part * width : (part + 1) * width], inv_z[:])
 
-            p_flipped_ps = [psum.tile([P, chunks, P], BF16, name=f"p_flipped_ps{part}", tag="bank") for part in parts]
+            p_flipped_ps.append([psum.tile([P, chunks, P], BF16, name=f"p_flipped_ps{part}", tag="bank") for part in parts])
+            fill_behind, fill_columns = (parts[-1], N) if blk < blocks[-1] else (0, P)
             for part in parts:
                 for k in range(chunks):
-                    nc.tensor.transpose(p_flipped_ps[part][:, k, :], p[part][:, k * P : (k + 1) * P], identity[:])
-            if blk < blocks[-1]:
-                nc.tensor.matmul(unread_ps[:], p[parts[-1]][:, 0:P], zero_columns, start=True, stop=True)
+                    nc.tensor.transpose(p_flipped_ps[blk][part][:, k, :], p[part][:, k * P : (k + 1) * P], identity[:])
+                if part == fill_behind:
+                    nc.tensor.matmul(
+                        unread_ps[:, 0:fill_columns], p[part][:, 0:P], zero_columns[:, 0:fill_columns], start=True, stop=True
+                    )
+
+        for blk in blocks:
+            chunks = chunks_in_part[blk]
+            parts = range(N // P // chunks)
             p_flipped = [work.tile([P, chunks, P], BF16, name=f"p_flipped{part}") for part in parts]
             for part in parts:
                 if blk < blocks[-1]:
-                    nc.scalar.copy(p_flipped[part][:], p_flipped_ps[part][:])
+                    nc.scalar.copy(p_flipped[part][:], p_flipped_ps[blk][part][:])
                 else:
-                    nc.vector.tensor_copy(p_flipped[part][:], p_flipped_ps[part][:])
+                    nc.vector.tensor_copy(p_flipped[part][:], p_flipped_ps[blk][part][:])
 
-            read_out = psum.tile([D, P], F32, name="read_out", tag="bank")
+            if blk < blocks[-1]:
+                read_out = psum_unread.tile([D, P], F32, name="read_out", tag="bank")
+            else:
+                read_out = psum.tile([D, P], F32, name="read_out", tag="bank")
             for part in parts:
                 for k in range(chunks):
                     chunk = part * chunks + k

@@ -52,17 +52,17 @@ def tile_base_kernel(tc, table, u, kmem, val, offs, out):
         pieces = range(N // PIECE)
         queries = [u_sb[:, blk * P : (blk + 1) * P] for blk in blocks]
         logits = [psum.tile([P, N], F32, name="logit", tag="bank") for blk in blocks]
-        nc.tensor.matmul(logits[0][:], queries[0], kmem_sb[:], start=True, stop=False)
+        for blk in blocks:
+            nc.tensor.matmul(logits[blk][:], queries[blk], kmem_sb[:], start=True, stop=False)
         for blk in blocks:
             for piece in pieces:
                 nc.tensor.matmul(
                     logits[blk][:, piece * PIECE : (piece + 1) * PIECE],
                     queries[blk],
                     table_cols[:].indirect(offsets[:, piece * PIECE // 16 : (piece + 1) * PIECE // 16]),
-                    start=(blk == 1 and piece == 0),
-                    stop=(blk == 0 and piece == pieces[-1]),
+                    start=False,
+                    stop=(piece == pieces[-1]),
                 )
-        nc.tensor.matmul(logits[1][:], queries[1], kmem_sb[:], start=False, stop=True)
 
         for i in range(LULL_FILLS):
             nc.tensor.matmul(unread_ps[:], table_cols[:, 0:P], zero_columns, start=True, stop=True)

@@ -32,7 +32,8 @@ def tile_base_kernel(tc, table, u, kmem, val, offs, out):
         make_identity(nc, identity[:])
 
         table_rows = held.tile([P, S // P, D], BF16, name="table_rows")
-        nc.sync.dma_start(table_rows[:], table.rearrange("(h p) d -> p h d", p=P))
+        nc.sync.dma_start(table_rows[:, 0, :], table[0:P, :])
+        nc.scalar.dma_start(table_rows[:, 1, :], table[P:S, :])
         u_sb = held.tile([D, B], BF16, name="u_sb")
         nc.sync.dma_start(u_sb[:], u)
         offsets = held.tile([P, N // 16], U16, name="offsets")

@@ -100,10 +100,7 @@ def tile_base_kernel(tc, table, u, kmem, val, offs, out):
             parts = range(N // P // chunks)
             p_flipped = [work.tile([P, chunks, P], BF16, name=f"p_flipped{part}") for part in parts]
             for part in parts:
-                if blk < blocks[-1]:
-                    nc.scalar.copy(p_flipped[part][:], p_flipped_ps[blk][part][:])
-                else:
-                    nc.vector.tensor_copy(p_flipped[part][:], p_flipped_ps[blk][part][:])
+                nc.vector.tensor_copy(p_flipped[part][:], p_flipped_ps[blk][part][:])
 
             if blk < blocks[-1]:
                 read_out = psum_unread.tile([D, P], F32, name="read_out", tag="bank")

@@ -36,12 +36,14 @@ def tile_base_kernel(tc, table, u, kmem, val, offs, out):
         nc.scalar.dma_start(table_rows[:, 1, :], table[P:S, :])
         u_sb = held.tile([D, B], BF16, name="u_sb")
         nc.sync.dma_start(u_sb[:], u)
+        HALF = N // 2
+        kmem_halves = [held.tile([D, HALF], BF16, name=f"kmem_half{half}") for half in range(2)]
+        for half, queue in enumerate([nc.scalar, nc.sync]):
+            queue.dma_start(kmem_halves[half][:], kmem[:, half * HALF : (half + 1) * HALF])
         offsets = held.tile([P, N // 16], U16, name="offsets")
         nc.sync.dma_start(offsets[:], offs)
-        kmem_sb = held.tile([D, N], BF16, name="kmem_sb")
-        nc.scalar.dma_start(kmem_sb[:], kmem)
         val_sb = held.tile([P, N // P, D], BF16, name="val_sb")
-        nc.sync.dma_start(val_sb[:], val.rearrange("(k p) d -> p k d", p=P))
+        nc.scalar.dma_start(val_sb[:], val.rearrange("(k p) d -> p k d", p=P))
 
         table_cols_ps = psum.tile([D, S], BF16, name="table_cols_ps", tag="bank")
         for h in range(S // P):
@@ -53,8 +55,11 @@ def tile_base_kernel(tc, table, u, kmem, val, offs, out):
         pieces = range(N // PIECE)
         queries = [u_sb[:, blk * P : (blk + 1) * P] for blk in blocks]
         logits = [psum.tile([P, N], F32, name="logit", tag="bank") for blk in blocks]
-        for blk in blocks:
-            nc.tensor.matmul(logits[blk][:], queries[blk], kmem_sb[:], start=True, stop=False)
+        for half, kmem_half in enumerate(kmem_halves):
+            for blk in blocks:
+                nc.tensor.matmul(
+                    logits[blk][:, half * HALF : (half + 1) * HALF], queries[blk], kmem_half[:], start=(half == 0), stop=False
+                )
         for blk in blocks:
             for piece in pieces:
                 nc.tensor.matmul(

@@ -32,18 +32,17 @@ def tile_base_kernel(tc, table, u, kmem, val, offs, out):
         make_identity(nc, identity[:])
 
         table_rows = held.tile([P, S // P, D], BF16, name="table_rows")
-        nc.sync.dma_start(table_rows[:, 0, :], table[0:P, :])
-        nc.scalar.dma_start(table_rows[:, 1, :], table[P:S, :])
+        nc.sync.dma_start(table_rows[:], table.rearrange("(h p) d -> p h d", p=P))
         u_sb = held.tile([D, B], BF16, name="u_sb")
-        nc.sync.dma_start(u_sb[:], u)
+        nc.scalar.dma_start(u_sb[:], u)
+        offsets = held.tile([P, N // 16], U16, name="offsets")
+        nc.sync.dma_start(offsets[:], offs)
         HALF = N // 2
         kmem_halves = [held.tile([D, HALF], BF16, name=f"kmem_half{half}") for half in range(2)]
         for half, queue in enumerate([nc.scalar, nc.sync]):
             queue.dma_start(kmem_halves[half][:], kmem[:, half * HALF : (half + 1) * HALF])
-        offsets = held.tile([P, N // 16], U16, name="offsets")
-        nc.sync.dma_start(offsets[:], offs)
         val_sb = held.tile([P, N // P, D], BF16, name="val_sb")
-        nc.scalar.dma_start(val_sb[:], val.rearrange("(k p) d -> p k d", p=P))
+        nc.sync.dma_start(val_sb[:], val.rearrange("(k p) d -> p k d", p=P))
 
         table_cols_ps = psum.tile([D, S], BF16, name="table_cols_ps", tag="bank")
         for h in range(S // P):

@@ -8,7 +8,7 @@ BF16, F32, U16 = mybir.dt.bfloat16, mybir.dt.float32, mybir.dt.uint16
 EXP = mybir.ActivationFunctionType.Exp
 ADD = mybir.AluOpType.add
 FLOPS = 3 * 2 * B * N * D
-WARM_UPS = 4
+WARM_UPS = 3
 LULL_FILLS = 5
 
 

import concourse.mybir as mybir
from concourse.masks import make_identity

P = 128
D, S, B, N = 128, 256, 256, 512
PIECE = 128
BF16, F32, U16 = mybir.dt.bfloat16, mybir.dt.float32, mybir.dt.uint16
EXP = mybir.ActivationFunctionType.Exp
ADD = mybir.AluOpType.add
FLOPS = 3 * 2 * B * N * D
WARM_UPS = 3
LULL_FILLS = 5


def tile_base_kernel(tc, table, u, kmem, val, offs, out):
    nc = tc.nc
    with (
        tc.tile_pool(name="held", bufs=1) as held,
        tc.tile_pool(name="work", bufs=2) as work,
        tc.psum_pool(name="psum", bufs=7) as psum,
        tc.psum_pool(name="psum_unread", bufs=1) as psum_unread,
    ):
        zero_column = held.tile([P, 1], BF16, name="zero_column")
        nc.gpsimd.memset(zero_column[:], 0.0)
        zero_weights = zero_column[:].to_broadcast([P, P])
        zero_columns = zero_column[:].to_broadcast([P, N])
        unread_ps = psum_unread.tile([P, N], F32, name="unread_ps", tag="bank")
        for i in range(WARM_UPS):
            nc.tensor.matmul(unread_ps[:], zero_weights, zero_columns, start=True, stop=True)

        identity = held.tile([P, P], BF16, name="identity")
        make_identity(nc, identity[:])

        table_rows = held.tile([P, S // P, D], BF16, name="table_rows")
        nc.sync.dma_start(table_rows[:], table.rearrange("(h p) d -> p h d", p=P))
        u_sb = held.tile([D, B], BF16, name="u_sb")
        nc.scalar.dma_start(u_sb[:], u)
        offsets = held.tile([P, N // 16], U16, name="offsets")
        nc.sync.dma_start(offsets[:], offs)
        HALF = N // 2
        kmem_halves = [held.tile([D, HALF], BF16, name=f"kmem_half{half}") for half in range(2)]
        for half, queue in enumerate([nc.scalar, nc.sync]):
            queue.dma_start(kmem_halves[half][:], kmem[:, half * HALF : (half + 1) * HALF])
        val_sb = held.tile([P, N // P, D], BF16, name="val_sb")
        nc.sync.dma_start(val_sb[:], val.rearrange("(k p) d -> p k d", p=P))

        table_cols_ps = psum.tile([D, S], BF16, name="table_cols_ps", tag="bank")
        for h in range(S // P):
            nc.tensor.transpose(table_cols_ps[:, h * P : (h + 1) * P], table_rows[:, h, :], identity[:])
        table_cols = held.tile([D, S], BF16, name="table_cols")
        nc.vector.tensor_copy(table_cols[:], table_cols_ps[:])

        blocks = range(B // P)
        pieces = range(N // PIECE)
        queries = [u_sb[:, blk * P : (blk + 1) * P] for blk in blocks]
        logits = [psum.tile([P, N], F32, name="logit", tag="bank") for blk in blocks]
        for half, kmem_half in enumerate(kmem_halves):
            for blk in blocks:
                nc.tensor.matmul(
                    logits[blk][:, half * HALF : (half + 1) * HALF], queries[blk], kmem_half[:], start=(half == 0), stop=False
                )
        for blk in blocks:
            for piece in pieces:
                nc.tensor.matmul(
                    logits[blk][:, piece * PIECE : (piece + 1) * PIECE],
                    queries[blk],
                    table_cols[:].indirect(offsets[:, piece * PIECE // 16 : (piece + 1) * PIECE // 16]),
                    start=False,
                    stop=(piece == pieces[-1]),
                )

        for i in range(LULL_FILLS):
            nc.tensor.matmul(unread_ps[:], table_cols[:, 0:P], zero_columns, start=True, stop=True)

        chunks_in_part = [2, 1]
        p_flipped_ps = []
        for blk in blocks:
            neg_max = work.tile([P, 1], F32, name="neg_max")
            nc.vector.reduce_max(neg_max[:], logits[blk][:], axis=mybir.AxisListType.X, negate=True)
            e = work.tile([P, N], F32, name="e")
            z = work.tile([P, 1], F32, name="z")
            nc.scalar.activation(e[:], logits[blk][:], EXP, bias=neg_max[:], accum_out=z[:])
            inv_z = work.tile([P, 1], F32, name="inv_z")
            nc.vector.reciprocal(inv_z[:], z[:])
            chunks = chunks_in_part[blk]
            width = chunks * P
            parts = range(N // width)
            p = [work.tile([P, width], BF16, name=f"p{part}") for part in parts]
            for part in parts:
                nc.vector.tensor_scalar_mul(p[part][:], e[:, part * width : (part + 1) * width], inv_z[:])

            p_flipped_ps.append([psum.tile([P, chunks, P], BF16, name=f"p_flipped_ps{part}", tag="bank") for part in parts])
            fill_behind, fill_columns = (parts[-1], N) if blk < blocks[-1] else (0, P)
            for part in parts:
                for k in range(chunks):
                    nc.tensor.transpose(p_flipped_ps[blk][part][:, k, :], p[part][:, k * P : (k + 1) * P], identity[:])
                if part == fill_behind:
                    nc.tensor.matmul(
                        unread_ps[:, 0:fill_columns], p[part][:, 0:P], zero_columns[:, 0:fill_columns], start=True, stop=True
                    )

        for blk in blocks:
            chunks = chunks_in_part[blk]
            parts = range(N // P // chunks)
            p_flipped = [work.tile([P, chunks, P], BF16, name=f"p_flipped{part}") for part in parts]
            for part in parts:
                nc.vector.tensor_copy(p_flipped[part][:], p_flipped_ps[blk][part][:])

            if blk < blocks[-1]:
                read_out = psum_unread.tile([D, P], F32, name="read_out", tag="bank")
            else:
                read_out = psum.tile([D, P], F32, name="read_out", tag="bank")
            for part in parts:
                for k in range(chunks):
                    chunk = part * chunks + k
                    nc.tensor.matmul(
                        read_out[:],
                        val_sb[:, chunk, :],
                        p_flipped[part][:, k, :],
                        start=(chunk == 0),
                        stop=(chunk == N // P - 1),
                    )
            out_sb = work.tile([D, P], F32, name="out_sb")
            nc.vector.tensor_tensor(out_sb[:], read_out[:], queries[blk], ADD)
            nc.sync.dma_start(out[:, blk * P : (blk + 1) * P], out_sb[:])
